import numpy as np
import ml_dtypes


def mxq(x, axis, fmt="e4m3"):
    dtype, down = {"e4m3": (ml_dtypes.float8_e4m3fn, 7), "e5m2": (ml_dtypes.float8_e5m2, 14)}[fmt]
    v = np.moveaxis(np.asarray(x, np.float32).astype(ml_dtypes.bfloat16).astype(np.float64), axis, -1)
    blocks = v.reshape(v.shape[:-1] + (-1, 32))
    amax = np.abs(blocks).max(-1, keepdims=True)
    byte = np.maximum(np.where(amax > 0, np.frexp(amax)[1] - 1 + 127, 0) - down, 1)
    scale = np.exp2(byte - 127.0)
    codes = (blocks / scale).astype(np.float32).astype(dtype).astype(np.float64)
    return np.moveaxis((codes * scale).reshape(v.shape), -1, axis)


WIDE = False


def mx_kscale(k):
    if not WIDE:
        return np.ones(k)
    levels = np.array([10, -10, 5, -5, 0])
    a = np.random.permutation(np.resize(levels, k // 512 * 4)).reshape(k // 512, 4)
    idx = np.arange(k)
    return np.exp2(a[idx // 512, idx % 128 // 32])


BF16 = ml_dtypes.bfloat16


def bf(x):
    return np.asarray(x, np.float32).astype(BF16)


def f64(x):
    return np.asarray(x).astype(np.float64)


B, S, IN_F, OUT_F, GROUP_SIZE = 4, 2048, 1024, 512, 128


def group_factors():
    u = np.unique(mx_kscale(IN_F))
    order = np.stack([u[::-1], u], 1).ravel()[:len(u)]
    return order[np.arange(IN_F // GROUP_SIZE) % len(u)]


def setup_inputs():
    g = group_factors()
    s = np.repeat(g, GROUP_SIZE)
    x = np.random.standard_normal((B, S, IN_F)) * s
    sw = np.random.standard_normal((OUT_F, IN_F))
    sw = np.where(sw == 0, 1.0, sw)
    scales = np.random.uniform(0.32, 3.2, OUT_F * IN_F // GROUP_SIZE) / np.sqrt(IN_F) / np.tile(g, OUT_F)
    return {"x": bf(x), "sign_weights": bf(sw), "scales": bf(scales)}


def reference(x, sign_weights, scales):
    binary = np.sign(f64(sign_weights))
    scale_mat = np.repeat(f64(scales), GROUP_SIZE).reshape(OUT_F, IN_F)
    weight = binary * scale_mat
    return mxq(f64(x), 2, "e4m3") @ mxq(weight, 1, "e4m3").T

@@ -1,0 +1,213 @@
+from contextlib import ExitStack
+
+import concourse.masks as masks
+import concourse.mybir as mybir
+
+FLOPS = 2 * 8192 * 1024 * 512
+
+F32 = mybir.dt.float32
+BF16 = mybir.dt.bfloat16
+U32 = mybir.dt.uint32
+U8 = mybir.dt.uint8
+FP8X4 = mybir.dt.float8_e4m3fn_x4
+ACT = mybir.ActivationFunctionType
+ALU = mybir.AluOpType
+
+P = 128
+K = 1024
+O = 512
+TOK = 8192
+J = 8
+NCH = TOK // (P * J)
+G = 2
+NG = TOK // (P * G)
+LAG = 2
+XB = 5
+MANUAL = False
+SORTED = True
+STORE_UNITS = [4] * 16
+
+
+def tile_stebitlinear_t_kernel(tc, x, sign_weights, scales, out):
+    nc = tc.nc
+    xv = x.flatten_outer_dims().rearrange("(h p j) k -> h p j k", p=P, j=J)
+    ov = out.flatten_outer_dims().rearrange("(h p j) o -> h p j o", p=P, j=J)
+
+    with ExitStack() as ctx:
+        if MANUAL:
+            ctx.enter_context(tc.manual_schedule())
+        const = ctx.enter_context(tc.tile_pool(name="const", bufs=1))
+        wprep = ctx.enter_context(tc.tile_pool(name="wprep", bufs=1))
+        xpool = ctx.enter_context(tc.tile_pool(name="xpool", bufs=XB))
+        spool = ctx.enter_context(tc.tile_pool(name="spool", bufs=4))
+        gpool = ctx.enter_context(tc.tile_pool(name="gpool", bufs=4))
+        cpool = ctx.enter_context(tc.tile_pool(name="cpool", bufs=LAG + 3))
+        opool = ctx.enter_context(tc.tile_pool(name="opool", bufs=4))
+        ps_t = ctx.enter_context(tc.psum_pool(name="ps_t", bufs=4))
+        ps_a = ctx.enter_context(tc.psum_pool(name="ps_a", bufs=4))
+
+        ident = const.tile([P, P], F32)
+        masks.make_identity(nc, ident[:])
+
+        sc = const.tile([P, 4, 16], BF16)
+        nc.sync.dma_start(out=sc[:, :, 0:8], in_=scales.rearrange("(t p g) -> p t g", t=4, p=P))
+        sw = wprep.tile([P, 4, K], BF16)
+        for t in range(4):
+            nc.sync.dma_start(out=sw[:, t, :], in_=sign_weights[t * P:(t + 1) * P, :])
+
+        xt = {}
+
+        def load(h):
+            x_sb = xpool.tile([P, J, K], BF16, name="x_sb")
+            xt[h] = x_sb
+            pieces = [(0, 2), (2, 4), (4, 8)] if h == 0 else [(0, J)]
+            for (a, b) in pieces:
+                nc.sync.dma_start(out=x_sb[:, a:b, :], in_=xv[h, :, a:b, :])
+
+        for h in range(XB):
+            load(h)
+
+        gw = wprep.tile([P, 2 * O * 4], BF16, align_bytes=64)
+        gwf = gw[:].bitcast(F32).rearrange("p (c t r u) -> p c t r u", c=2, t=4, u=2)
+        for t in range(4):
+            sg = wprep.tile([P, K], BF16, tag="sg", bufs=2)
+            nc.scalar.activation(out=sg[:], in_=sw[:, t, :], func=ACT.Sign)
+            wn = wprep.tile([P, K], BF16, tag="wn", bufs=4)
+            nc.vector.tensor_tensor(
+                out=wn[:].rearrange("p (g w) -> p g w", g=8),
+                in0=sg[:].rearrange("p (g w) -> p g w", g=8),
+                in1=sc[:, t, 0:8].unsqueeze(2).to_broadcast([P, 8, P]),
+                op=ALU.mult,
+            )
+            wv = wn[:].bitcast(F32).rearrange("p (c w u) -> p c u w", c=2, u=2)
+            w_t = ps_t.tile([P, 2, 2, P], F32, tag="bank_t")
+            for c in range(2):
+                for u in range(2):
+                    nc.tensor.transpose(w_t[:, c, u, :], wv[:, c, u, :], ident[:])
+            src = w_t[:].rearrange("p c u r -> p c r u")
+            if t % 2 == 0:
+                nc.vector.tensor_copy(out=gwf[:, :, t, :, :], in_=src)
+            else:
+                nc.scalar.copy(out=gwf[:, :, t, :, :], in_=src)
+        w_codes = const.tile([P, 2 * O], U32, align_bytes=64)
+        w_scl = const.tile([P, 2 * O], U8, align_bytes=64)
+        nc.vector.quantize_mx(out=w_codes[:].bitcast(FP8X4), scales=w_scl[:], in_=gw[:])
+
+        srt_of = {}
+        bank_of = {}
+        grp_of = {}
+        code_of = {}
+        acc_of = {}
+
+        def where(g):
+            return (g * G) // J, (g * G) % J
+
+        def sort(g):
+            h, j0 = where(g)
+            srt = spool.tile([P, G * 2, 2, P], F32, name="srt")
+            nc.vector.tensor_copy(
+                out=srt[:],
+                in_=xt[h][:].bitcast(F32)[:, j0:j0 + G, :].rearrange(
+                    "p n (c w u) -> p (n c) u w", c=2, u=2),
+            )
+            srt_of[g] = srt
+
+        def transposes(g):
+            h, j0 = where(g)
+            banks = []
+            for n in range(G):
+                bank = ps_t.tile([P, 2, 2, P], F32, tag="bank_t", name="bank")
+                for c in range(2):
+                    for u in range(2):
+                        if SORTED:
+                            src = srt_of[g][:, n * 2 + c, u, :]
+                        else:
+                            src = xt[h][:].bitcast(F32)[:, j0 + n, :].rearrange(
+                                "p (c w u) -> p c u w", c=2, u=2)[:, c, u, :]
+                        nc.tensor.transpose(bank[:, c, u, :], src, ident[:])
+                banks.append(bank)
+            bank_of[g] = banks
+
+        def copies(g):
+            grp = gpool.tile([P, G * K], BF16, align_bytes=64, name="grp")
+            gf = grp[:].bitcast(F32).rearrange("p (n c r u) -> p n c r u", n=G, c=2, u=2)
+            for n in range(G):
+                src = bank_of[g][n][:].rearrange("p c u r -> p c r u")
+                if n % 2 == 0:
+                    nc.vector.tensor_copy(out=gf[:, n], in_=src)
+                else:
+                    nc.scalar.copy(out=gf[:, n], in_=src)
+            grp_of[g] = grp
+
+        def quantise(g):
+            codes = cpool.tile([P, G * 2 * P], U32, align_bytes=64, name="codes")
+            scl = cpool.tile([P, G * 2 * P], U8, align_bytes=64, name="scl")
+            nc.vector.quantize_mx(out=codes[:].bitcast(FP8X4), scales=scl[:], in_=grp_of[g][:])
+            code_of[g] = (codes, scl)
+
+        def passes(g):
+            codes, scl = code_of[g]
+            accs = []
+            for n in range(G):
+                acc = ps_a.tile([P, O], F32, name="acc")
+                for c in range(2):
+                    cols = slice((n * 2 + c) * P, (n * 2 + c + 1) * P)
+                    nc.tensor.matmul_mx(
+                        out=acc[:],
+                        lhsT=codes[:, cols].bitcast(FP8X4),
+                        lhsT_scale=scl[:, cols],
+                        rhs=w_codes[:, c * O:(c + 1) * O].bitcast(FP8X4),
+                        rhs_scale=w_scl[:, c * O:(c + 1) * O],
+                        start=(c == 0),
+                        stop=(c == 1),
+                    )
+                accs.append(acc)
+            acc_of[g] = accs
+
+        unit_start = []
+        s = 0
+        for n_tiles in STORE_UNITS:
+            unit_start.append(s)
+            s += n_tiles
+        assert s == TOK // P
+        stage = {}
+
+        def results(g):
+            for n in range(G):
+                tile_no = g * G + n
+                if tile_no in unit_start:
+                    width = STORE_UNITS[unit_start.index(tile_no)]
+                    o_sb = opool.tile([P, 4, O], F32, name="o_sb")
+                    stage["tile"] = o_sb
+                    stage["first"] = tile_no
+                    stage["width"] = width
+                o_sb = stage["tile"]
+                k = tile_no - stage["first"]
+                nc.scalar.copy(out=o_sb[:, k, :], in_=acc_of[g][n][:])
+                if k == stage["width"] - 1:
+                    h = stage["first"] // J
+                    j0 = stage["first"] % J
+                    nc.scalar.dma_start(out=ov[h, :, j0:j0 + k + 1, :], in_=o_sb[:, 0:k + 1, :])
+
+        if SORTED:
+            sort(0)
+            sort(1)
+        for i in range(NG + LAG):
+            if i < NG:
+                transposes(i)
+            if 1 <= i <= NG:
+                quantise(i - 1)
+            if SORTED and i + 2 < NG:
+                h, j0 = where(i + 2)
+                sort(i + 2)
+                if j0 + G == J and h + XB < NCH:
+                    load(h + XB)
+            if i < NG:
+                copies(i)
+                if not SORTED:
+                    h, j0 = where(i)
+                    if j0 + G == J and h + XB < NCH:
+                        load(h + XB)
+            if LAG <= i < NG + LAG:
+                passes(i - LAG)
+                results(i - LAG)

@@ -23,7 +23,7 @@ G = 2
 NG = TOK // (P * G)
 LAG = 2
 XB = 5
-MANUAL = False
+MANUAL = True
 SORTED = True
 STORE_UNITS = [4] * 16
 
@@ -69,29 +69,38 @@ def tile_stebitlinear_t_kernel(tc, x, sign_weights, scales, out):
 
         gw = wprep.tile([P, 2 * O * 4], BF16, align_bytes=64)
         gwf = gw[:].bitcast(F32).rearrange("p (c t r u) -> p c t r u", c=2, t=4, u=2)
-        for t in range(4):
-            sg = wprep.tile([P, K], BF16, tag="sg", bufs=2)
+        sg_of = {}
+        wt_of = {}
+
+        def w_sign(t):
+            sg = wprep.tile([P, K], BF16, tag="sg", bufs=4, name="sg")
             nc.scalar.activation(out=sg[:], in_=sw[:, t, :], func=ACT.Sign)
-            wn = wprep.tile([P, K], BF16, tag="wn", bufs=4)
+            sg_of[t] = sg
+
+        def w_scale_and_transpose(t):
+            wn = wprep.tile([P, K], BF16, tag="wn", bufs=4, name="wn")
             nc.vector.tensor_tensor(
                 out=wn[:].rearrange("p (g w) -> p g w", g=8),
-                in0=sg[:].rearrange("p (g w) -> p g w", g=8),
+                in0=sg_of[t][:].rearrange("p (g w) -> p g w", g=8),
                 in1=sc[:, t, 0:8].unsqueeze(2).to_broadcast([P, 8, P]),
                 op=ALU.mult,
             )
             wv = wn[:].bitcast(F32).rearrange("p (c w u) -> p c u w", c=2, u=2)
-            w_t = ps_t.tile([P, 2, 2, P], F32, tag="bank_t")
+            w_t = ps_t.tile([P, 2, 2, P], F32, tag="bank_t", name="w_t")
             for c in range(2):
                 for u in range(2):
                     nc.tensor.transpose(w_t[:, c, u, :], wv[:, c, u, :], ident[:])
-            src = w_t[:].rearrange("p c u r -> p c r u")
-            if t % 2 == 0:
+            wt_of[t] = w_t
+
+        def w_copy(t, on_vector):
+            src = wt_of[t][:].rearrange("p c u r -> p c r u")
+            if on_vector:
                 nc.vector.tensor_copy(out=gwf[:, :, t, :, :], in_=src)
             else:
                 nc.scalar.copy(out=gwf[:, :, t, :, :], in_=src)
+
         w_codes = const.tile([P, 2 * O], U32, align_bytes=64)
         w_scl = const.tile([P, 2 * O], U8, align_bytes=64)
-        nc.vector.quantize_mx(out=w_codes[:].bitcast(FP8X4), scales=w_scl[:], in_=gw[:])
 
         srt_of = {}
         bank_of = {}
@@ -187,11 +196,19 @@ def tile_stebitlinear_t_kernel(tc, x, sign_weights, scales, out):
                 if k == stage["width"] - 1:
                     h = stage["first"] // J
                     j0 = stage["first"] % J
-                    nc.scalar.dma_start(out=ov[h, :, j0:j0 + k + 1, :], in_=o_sb[:, 0:k + 1, :])
+                    nc.gpsimd.dma_start(out=ov[h, :, j0:j0 + k + 1, :], in_=o_sb[:, 0:k + 1, :])
 
+        for t in range(4):
+            w_sign(t)
+        for t in range(4):
+            w_scale_and_transpose(t)
+            if t > 0:
+                w_copy(t - 1, t - 1 < 2)
         if SORTED:
             sort(0)
             sort(1)
+        w_copy(3, False)
+        nc.vector.quantize_mx(out=w_codes[:].bitcast(FP8X4), scales=w_scl[:], in_=gw[:])
         for i in range(NG + LAG):
             if i < NG:
                 transposes(i)

@@ -78,14 +78,19 @@ def tile_stebitlinear_t_kernel(tc, x, sign_weights, scales, out):
             sg_of[t] = sg
 
         def w_scale_and_transpose(t):
-            wn = wprep.tile([P, K], BF16, tag="wn", bufs=4, name="wn")
+            wn = wprep.tile([P, K], BF16, tag="wn", bufs=2, name="wn")
             nc.vector.tensor_tensor(
                 out=wn[:].rearrange("p (g w) -> p g w", g=8),
                 in0=sg_of[t][:].rearrange("p (g w) -> p g w", g=8),
                 in1=sc[:, t, 0:8].unsqueeze(2).to_broadcast([P, 8, P]),
                 op=ALU.mult,
             )
-            wv = wn[:].bitcast(F32).rearrange("p (c w u) -> p c u w", c=2, u=2)
+            ws = wprep.tile([P, 2, 2, 2 * P], BF16, tag="ws", bufs=4, name="ws")
+            nc.vector.tensor_copy(
+                out=ws[:].rearrange("p c u (a i) -> p c u a i", i=16),
+                in_=wn[:].rearrange("p (c a u i) -> p c u a i", c=2, u=2, i=16),
+            )
+            wv = ws[:].bitcast(F32)
             w_t = ps_t.tile([P, 2, 2, P], F32, tag="bank_t", name="w_t")
             for c in range(2):
                 for u in range(2):
@@ -113,13 +118,13 @@ def tile_stebitlinear_t_kernel(tc, x, sign_weights, scales, out):
 
         def sort(g):
             h, j0 = where(g)
-            srt = spool.tile([P, G * 2, 2, P], F32, name="srt")
+            srt = spool.tile([P, G * 2, 2, 2 * P], BF16, name="srt")
             nc.vector.tensor_copy(
-                out=srt[:],
-                in_=xt[h][:].bitcast(F32)[:, j0:j0 + G, :].rearrange(
-                    "p n (c w u) -> p (n c) u w", c=2, u=2),
+                out=srt[:].rearrange("p m u (a i) -> p m u a i", i=16),
+                in_=xt[h][:, j0:j0 + G, :].rearrange(
+                    "p n (c a u i) -> p (n c) u a i", c=2, u=2, i=16),
             )
-            srt_of[g] = srt
+            srt_of[g] = srt[:].bitcast(F32)
 
         def transposes(g):
             h, j0 = where(g)

@@ -25,7 +25,7 @@ LAG = 2
 XB = 5
 MANUAL = True
 SORTED = True
-STORE_UNITS = [4] * 16
+STORE_UNITS = [4] * 15 + [2, 1, 1]
 
 
 def tile_stebitlinear_t_kernel(tc, x, sign_weights, scales, out):
@@ -197,11 +197,16 @@ def tile_stebitlinear_t_kernel(tc, x, sign_weights, scales, out):
                     stage["width"] = width
                 o_sb = stage["tile"]
                 k = tile_no - stage["first"]
-                nc.scalar.copy(out=o_sb[:, k, :], in_=acc_of[g][n][:])
+                at_end = tile_no >= TOK // P - 4
+                if at_end and n % 2 == 0:
+                    nc.vector.tensor_copy(out=o_sb[:, k, :], in_=acc_of[g][n][:])
+                else:
+                    nc.scalar.copy(out=o_sb[:, k, :], in_=acc_of[g][n][:])
                 if k == stage["width"] - 1:
                     h = stage["first"] // J
                     j0 = stage["first"] % J
-                    nc.gpsimd.dma_start(out=ov[h, :, j0:j0 + k + 1, :], in_=o_sb[:, 0:k + 1, :])
+                    queue = nc.sync if at_end else nc.scalar
+                    queue.dma_start(out=ov[h, :, j0:j0 + k + 1, :], in_=o_sb[:, 0:k + 1, :])
 
         for t in range(4):
             w_sign(t)

@@ -17,14 +17,12 @@ P = 128
 K = 1024
 O = 512
 TOK = 8192
+TILES = TOK // P
 J = 8
-NCH = TOK // (P * J)
-G = 2
-NG = TOK // (P * G)
-LAG = 2
-XB = 5
-MANUAL = True
-SORTED = True
+NCH = TILES // J
+G = 4
+NG = TILES // G
+XB = 4
 STORE_UNITS = [4] * 15 + [2, 1, 1]
 
 
@@ -34,17 +32,15 @@ def tile_stebitlinear_t_kernel(tc, x, sign_weights, scales, out):
     ov = out.flatten_outer_dims().rearrange("(h p j) o -> h p j o", p=P, j=J)
 
     with ExitStack() as ctx:
-        if MANUAL:
-            ctx.enter_context(tc.manual_schedule())
+        ctx.enter_context(tc.manual_schedule())
         const = ctx.enter_context(tc.tile_pool(name="const", bufs=1))
         wprep = ctx.enter_context(tc.tile_pool(name="wprep", bufs=1))
         xpool = ctx.enter_context(tc.tile_pool(name="xpool", bufs=XB))
-        spool = ctx.enter_context(tc.tile_pool(name="spool", bufs=4))
-        gpool = ctx.enter_context(tc.tile_pool(name="gpool", bufs=4))
-        cpool = ctx.enter_context(tc.tile_pool(name="cpool", bufs=LAG + 3))
+        spool = ctx.enter_context(tc.tile_pool(name="spool", bufs=3))
+        gpool = ctx.enter_context(tc.tile_pool(name="gpool", bufs=3))
+        cpool = ctx.enter_context(tc.tile_pool(name="cpool", bufs=4))
         opool = ctx.enter_context(tc.tile_pool(name="opool", bufs=4))
-        ps_t = ctx.enter_context(tc.psum_pool(name="ps_t", bufs=4))
-        ps_a = ctx.enter_context(tc.psum_pool(name="ps_a", bufs=4))
+        psum = ctx.enter_context(tc.psum_pool(name="psum", bufs=8))
 
         ident = const.tile([P, P], F32)
         masks.make_identity(nc, ident[:])
@@ -69,6 +65,8 @@ def tile_stebitlinear_t_kernel(tc, x, sign_weights, scales, out):
 
         gw = wprep.tile([P, 2 * O * 4], BF16, align_bytes=64)
         gwf = gw[:].bitcast(F32).rearrange("p (c t r u) -> p c t r u", c=2, t=4, u=2)
+        w_codes = const.tile([P, 2 * O], U32, align_bytes=64)
+        w_scl = const.tile([P, 2 * O], U8, align_bytes=64)
         sg_of = {}
         wt_of = {}
 
@@ -91,63 +89,63 @@ def tile_stebitlinear_t_kernel(tc, x, sign_weights, scales, out):
                 in_=wn[:].rearrange("p (c a u i) -> p c u a i", c=2, u=2, i=16),
             )
             wv = ws[:].bitcast(F32)
-            w_t = ps_t.tile([P, 2, 2, P], F32, tag="bank_t", name="w_t")
+            w_t = psum.tile([P, 2, 2, P], F32, tag="bank", name="w_t")
             for c in range(2):
                 for u in range(2):
                     nc.tensor.transpose(w_t[:, c, u, :], wv[:, c, u, :], ident[:])
             wt_of[t] = w_t
 
-        def w_copy(t, on_vector):
-            src = wt_of[t][:].rearrange("p c u r -> p c r u")
-            if on_vector:
-                nc.vector.tensor_copy(out=gwf[:, :, t, :, :], in_=src)
-            else:
-                nc.scalar.copy(out=gwf[:, :, t, :, :], in_=src)
-
-        w_codes = const.tile([P, 2 * O], U32, align_bytes=64)
-        w_scl = const.tile([P, 2 * O], U8, align_bytes=64)
+        def w_copy_and_quantise(t):
+            nc.scalar.copy(out=gwf[:, :, t, :, :], in_=wt_of[t][:].rearrange("p c u r -> p c r u"))
+            for c in range(2):
+                first = c * O + t * P
+                nc.vector.quantize_mx(
+                    out=w_codes[:, first:first + P].bitcast(FP8X4),
+                    scales=w_scl[:, first:first + P],
+                    in_=gw[:, first * 4:(first + P) * 4],
+                )
 
         srt_of = {}
         bank_of = {}
         grp_of = {}
         code_of = {}
         acc_of = {}
+        next_load = [XB]
 
-        def where(g):
-            return (g * G) // J, (g * G) % J
-
-        def sort(g):
-            h, j0 = where(g)
+        def sort(g, pieces):
+            h = (g * G) // J
+            j0 = (g * G) % J
             srt = spool.tile([P, G * 2, 2, 2 * P], BF16, name="srt")
-            nc.vector.tensor_copy(
-                out=srt[:].rearrange("p m u (a i) -> p m u a i", i=16),
-                in_=xt[h][:, j0:j0 + G, :].rearrange(
-                    "p n (c a u i) -> p (n c) u a i", c=2, u=2, i=16),
-            )
             srt_of[g] = srt[:].bitcast(F32)
+            moves = []
+            for (a, b) in pieces:
+                moves.append((
+                    srt[:, 2 * a:2 * b, :, :].rearrange("p m u (a i) -> p m u a i", i=16),
+                    xt[h][:, j0 + a:j0 + b, :].rearrange(
+                        "p n (c a u i) -> p (n c) u a i", c=2, u=2, i=16),
+                ))
+            return moves
 
-        def transposes(g):
-            h, j0 = where(g)
-            banks = []
-            for n in range(G):
-                bank = ps_t.tile([P, 2, 2, P], F32, tag="bank_t", name="bank")
-                for c in range(2):
-                    for u in range(2):
-                        if SORTED:
-                            src = srt_of[g][:, n * 2 + c, u, :]
-                        else:
-                            src = xt[h][:].bitcast(F32)[:, j0 + n, :].rearrange(
-                                "p (c w u) -> p c u w", c=2, u=2)[:, c, u, :]
-                        nc.tensor.transpose(bank[:, c, u, :], src, ident[:])
-                banks.append(bank)
-            bank_of[g] = banks
+        def sort_whole(g):
+            for (dst, src) in sort(g, [(0, G)]):
+                nc.vector.tensor_copy(out=dst, in_=src)
+            if (g * G + G) % J == 0 and next_load[0] < NCH:
+                load(next_load[0])
+                next_load[0] += 1
 
-        def copies(g):
+        def transposes(g, n):
+            bank = psum.tile([P, 2, 2, P], F32, tag="bank", name="bank")
+            for c in range(2):
+                for u in range(2):
+                    nc.tensor.transpose(bank[:, c, u, :], srt_of[g][:, n * 2 + c, u, :], ident[:])
+            bank_of[(g, n)] = bank
+
+        def copies(g, all_on_scalar):
             grp = gpool.tile([P, G * K], BF16, align_bytes=64, name="grp")
             gf = grp[:].bitcast(F32).rearrange("p (n c r u) -> p n c r u", n=G, c=2, u=2)
             for n in range(G):
-                src = bank_of[g][n][:].rearrange("p c u r -> p c r u")
-                if n % 2 == 0:
+                src = bank_of[(g, n)][:].rearrange("p c u r -> p c r u")
+                if n % 2 == 0 and not all_on_scalar:
                     nc.vector.tensor_copy(out=gf[:, n], in_=src)
                 else:
                     nc.scalar.copy(out=gf[:, n], in_=src)
@@ -163,7 +161,7 @@ def tile_stebitlinear_t_kernel(tc, x, sign_weights, scales, out):
             codes, scl = code_of[g]
             accs = []
             for n in range(G):
-                acc = ps_a.tile([P, O], F32, name="acc")
+                acc = psum.tile([P, O], F32, tag="bank", name="acc")
                 for c in range(2):
                     cols = slice((n * 2 + c) * P, (n * 2 + c + 1) * P)
                     nc.tensor.matmul_mx(
@@ -183,21 +181,20 @@ def tile_stebitlinear_t_kernel(tc, x, sign_weights, scales, out):
         for n_tiles in STORE_UNITS:
             unit_start.append(s)
             s += n_tiles
-        assert s == TOK // P
+        assert s == TILES
         stage = {}
 
         def results(g):
             for n in range(G):
                 tile_no = g * G + n
                 if tile_no in unit_start:
-                    width = STORE_UNITS[unit_start.index(tile_no)]
                     o_sb = opool.tile([P, 4, O], F32, name="o_sb")
                     stage["tile"] = o_sb
                     stage["first"] = tile_no
-                    stage["width"] = width
+                    stage["width"] = STORE_UNITS[unit_start.index(tile_no)]
                 o_sb = stage["tile"]
                 k = tile_no - stage["first"]
-                at_end = tile_no >= TOK // P - 4
+                at_end = tile_no >= TILES - 4
                 if at_end and n % 2 == 0:
                     nc.vector.tensor_copy(out=o_sb[:, k, :], in_=acc_of[g][n][:])
                 else:
@@ -210,31 +207,29 @@ def tile_stebitlinear_t_kernel(tc, x, sign_weights, scales, out):
 
         for t in range(4):
             w_sign(t)
-        for t in range(4):
+        for t in range(3):
             w_scale_and_transpose(t)
-            if t > 0:
-                w_copy(t - 1, t - 1 < 2)
-        if SORTED:
-            sort(0)
-            sort(1)
-        w_copy(3, False)
-        nc.vector.quantize_mx(out=w_codes[:].bitcast(FP8X4), scales=w_scl[:], in_=gw[:])
-        for i in range(NG + LAG):
+        halves = sort(0, [(0, 2), (2, 4)])
+        nc.vector.tensor_copy(out=halves[0][0], in_=halves[0][1])
+        transposes(0, 0)
+        transposes(0, 1)
+        w_scale_and_transpose(3)
+        nc.vector.tensor_copy(out=halves[1][0], in_=halves[1][1])
+        transposes(0, 2)
+        transposes(0, 3)
+        for t in range(4):
+            w_copy_and_quantise(t)
+        copies(0, True)
+        sort_whole(1)
+
+        for i in range(1, NG + 1):
             if i < NG:
-                transposes(i)
-            if 1 <= i <= NG:
-                quantise(i - 1)
-            if SORTED and i + 2 < NG:
-                h, j0 = where(i + 2)
-                sort(i + 2)
-                if j0 + G == J and h + XB < NCH:
-                    load(h + XB)
+                for n in range(G):
+                    transposes(i, n)
+            quantise(i - 1)
+            if i + 1 < NG:
+                sort_whole(i + 1)
             if i < NG:
-                copies(i)
-                if not SORTED:
-                    h, j0 = where(i)
-                    if j0 + G == J and h + XB < NCH:
-                        load(h + XB)
-            if LAG <= i < NG + LAG:
-                passes(i - LAG)
-                results(i - LAG)
+                copies(i, False)
+            passes(i - 1)
+            results(i - 1)

@@ -21,13 +21,14 @@ TILES = TOK // P
 J = 8
 NCH = TILES // J
 G = 4
-NG = TILES // G
+NQ = TILES // G
 XB = 4
 STORE_UNITS = [4] * 15 + [2, 1, 1]
 
 
 def tile_stebitlinear_t_kernel(tc, x, sign_weights, scales, out):
     nc = tc.nc
+    GROUPS = [[0], [1]] + [[q, q + 1] for q in range(2, NQ, 2)]
     xv = x.flatten_outer_dims().rearrange("(h p j) k -> h p j k", p=P, j=J)
     ov = out.flatten_outer_dims().rearrange("(h p j) o -> h p j o", p=P, j=J)
 
@@ -36,7 +37,7 @@ def tile_stebitlinear_t_kernel(tc, x, sign_weights, scales, out):
         const = ctx.enter_context(tc.tile_pool(name="const", bufs=1))
         wprep = ctx.enter_context(tc.tile_pool(name="wprep", bufs=1))
         xpool = ctx.enter_context(tc.tile_pool(name="xpool", bufs=XB))
-        spool = ctx.enter_context(tc.tile_pool(name="spool", bufs=3))
+        spool = ctx.enter_context(tc.tile_pool(name="spool", bufs=4))
         gpool = ctx.enter_context(tc.tile_pool(name="gpool", bufs=3))
         cpool = ctx.enter_context(tc.tile_pool(name="cpool", bufs=4))
         opool = ctx.enter_context(tc.tile_pool(name="opool", bufs=4))
@@ -221,15 +222,21 @@ def tile_stebitlinear_t_kernel(tc, x, sign_weights, scales, out):
             w_copy_and_quantise(t)
         copies(0, True)
         sort_whole(1)
+        quantise(0)
 
-        for i in range(1, NG + 1):
-            if i < NG:
+        for i in range(1, len(GROUPS) + 1):
+            now = GROUPS[i] if i < len(GROUPS) else []
+            after = GROUPS[i + 1] if i + 1 < len(GROUPS) else []
+            for q in now:
                 for n in range(G):
-                    transposes(i, n)
-            quantise(i - 1)
-            if i + 1 < NG:
-                sort_whole(i + 1)
-            if i < NG:
-                copies(i, False)
-            passes(i - 1)
-            results(i - 1)
+                    transposes(q, n)
+            for q in now:
+                copies(q, False)
+            for q in GROUPS[i - 1]:
+                passes(q)
+            for q in after:
+                sort_whole(q)
+            for q in now:
+                quantise(q)
+            for q in GROUPS[i - 1]:
+                results(q)

@@ -21,14 +21,13 @@ TILES = TOK // P
 J = 8
 NCH = TILES // J
 G = 4
-NQ = TILES // G
+NG = TILES // G
 XB = 4
 STORE_UNITS = [4] * 15 + [2, 1, 1]
 
 
 def tile_stebitlinear_t_kernel(tc, x, sign_weights, scales, out):
     nc = tc.nc
-    GROUPS = [[0], [1]] + [[q, q + 1] for q in range(2, NQ, 2)]
     xv = x.flatten_outer_dims().rearrange("(h p j) k -> h p j k", p=P, j=J)
     ov = out.flatten_outer_dims().rearrange("(h p j) o -> h p j o", p=P, j=J)
 
@@ -37,7 +36,7 @@ def tile_stebitlinear_t_kernel(tc, x, sign_weights, scales, out):
         const = ctx.enter_context(tc.tile_pool(name="const", bufs=1))
         wprep = ctx.enter_context(tc.tile_pool(name="wprep", bufs=1))
         xpool = ctx.enter_context(tc.tile_pool(name="xpool", bufs=XB))
-        spool = ctx.enter_context(tc.tile_pool(name="spool", bufs=4))
+        spool = ctx.enter_context(tc.tile_pool(name="spool", bufs=3))
         gpool = ctx.enter_context(tc.tile_pool(name="gpool", bufs=3))
         cpool = ctx.enter_context(tc.tile_pool(name="cpool", bufs=4))
         opool = ctx.enter_context(tc.tile_pool(name="opool", bufs=4))
@@ -48,6 +47,8 @@ def tile_stebitlinear_t_kernel(tc, x, sign_weights, scales, out):
 
         sc = const.tile([P, 4, 16], BF16)
         nc.sync.dma_start(out=sc[:, :, 0:8], in_=scales.rearrange("(t p g) -> p t g", t=4, p=P))
+        scf = const.tile([P, 4, 8], F32)
+        nc.vector.tensor_copy(out=scf[:], in_=sc[:, :, 0:8])
         sw = wprep.tile([P, 4, K], BF16)
         for t in range(4):
             nc.sync.dma_start(out=sw[:, t, :], in_=sign_weights[t * P:(t + 1) * P, :])
@@ -77,18 +78,15 @@ def tile_stebitlinear_t_kernel(tc, x, sign_weights, scales, out):
             sg_of[t] = sg
 
         def w_scale_and_transpose(t):
-            wn = wprep.tile([P, K], BF16, tag="wn", bufs=2, name="wn")
-            nc.vector.tensor_tensor(
-                out=wn[:].rearrange("p (g w) -> p g w", g=8),
-                in0=sg_of[t][:].rearrange("p (g w) -> p g w", g=8),
-                in1=sc[:, t, 0:8].unsqueeze(2).to_broadcast([P, 8, P]),
-                op=ALU.mult,
-            )
             ws = wprep.tile([P, 2, 2, 2 * P], BF16, tag="ws", bufs=4, name="ws")
-            nc.vector.tensor_copy(
-                out=ws[:].rearrange("p c u (a i) -> p c u a i", i=16),
-                in_=wn[:].rearrange("p (c a u i) -> p c u a i", c=2, u=2, i=16),
-            )
+            for g in range(8):
+                c = g // 4
+                a0 = (g % 4) * 64
+                nc.vector.tensor_scalar_mul(
+                    out=ws[:, c, :, a0:a0 + 64].rearrange("p u (a i) -> p a u i", i=16),
+                    in0=sg_of[t][:, g * P:(g + 1) * P].rearrange("p (a u i) -> p a u i", u=2, i=16),
+                    scalar1=scf[:, t, g:g + 1],
+                )
             wv = ws[:].bitcast(F32)
             w_t = psum.tile([P, 2, 2, P], F32, tag="bank", name="w_t")
             for c in range(2):
@@ -96,8 +94,10 @@ def tile_stebitlinear_t_kernel(tc, x, sign_weights, scales, out):
                     nc.tensor.transpose(w_t[:, c, u, :], wv[:, c, u, :], ident[:])
             wt_of[t] = w_t
 
-        def w_copy_and_quantise(t):
+        def w_copy(t):
             nc.scalar.copy(out=gwf[:, :, t, :, :], in_=wt_of[t][:].rearrange("p c u r -> p c r u"))
+
+        def w_quantise(t):
             for c in range(2):
                 first = c * O + t * P
                 nc.vector.quantize_mx(
@@ -141,21 +141,30 @@ def tile_stebitlinear_t_kernel(tc, x, sign_weights, scales, out):
                     nc.tensor.transpose(bank[:, c, u, :], srt_of[g][:, n * 2 + c, u, :], ident[:])
             bank_of[(g, n)] = bank
 
-        def copies(g, all_on_scalar):
-            grp = gpool.tile([P, G * K], BF16, align_bytes=64, name="grp")
-            gf = grp[:].bitcast(F32).rearrange("p (n c r u) -> p n c r u", n=G, c=2, u=2)
-            for n in range(G):
-                src = bank_of[(g, n)][:].rearrange("p c u r -> p c r u")
-                if n % 2 == 0 and not all_on_scalar:
-                    nc.vector.tensor_copy(out=gf[:, n], in_=src)
-                else:
-                    nc.scalar.copy(out=gf[:, n], in_=src)
-            grp_of[g] = grp
+        def copy_out(g, n, on_vector):
+            if n == 0:
+                grp = gpool.tile([P, G * K], BF16, align_bytes=64, name="grp")
+                grp_of[g] = grp
+            gf = grp_of[g][:].bitcast(F32).rearrange("p (n c r u) -> p n c r u", n=G, c=2, u=2)
+            src = bank_of[(g, n)][:].rearrange("p c u r -> p c r u")
+            if on_vector:
+                nc.vector.tensor_copy(out=gf[:, n], in_=src)
+            else:
+                nc.scalar.copy(out=gf[:, n], in_=src)
 
-        def quantise(g):
+        def copies(g):
+            for n in range(G):
+                copy_out(g, n, n % 2 == 0)
+
+        def quantise(g, pieces):
             codes = cpool.tile([P, G * 2 * P], U32, align_bytes=64, name="codes")
             scl = cpool.tile([P, G * 2 * P], U8, align_bytes=64, name="scl")
-            nc.vector.quantize_mx(out=codes[:].bitcast(FP8X4), scales=scl[:], in_=grp_of[g][:])
+            for (a, b) in pieces:
+                nc.vector.quantize_mx(
+                    out=codes[:, a * 2 * P:b * 2 * P].bitcast(FP8X4),
+                    scales=scl[:, a * 2 * P:b * 2 * P],
+                    in_=grp_of[g][:, a * K:b * K],
+                )
             code_of[g] = (codes, scl)
 
         def passes(g):
@@ -218,25 +227,29 @@ def tile_stebitlinear_t_kernel(tc, x, sign_weights, scales, out):
         nc.vector.tensor_copy(out=halves[1][0], in_=halves[1][1])
         transposes(0, 2)
         transposes(0, 3)
-        for t in range(4):
-            w_copy_and_quantise(t)
-        copies(0, True)
+        for t in range(3):
+            w_copy(t)
+        copy_out(0, 0, False)
+        copy_out(0, 1, False)
+        w_copy(3)
+        copy_out(0, 2, False)
+        copy_out(0, 3, False)
+        w_quantise(0)
+        w_quantise(1)
         sort_whole(1)
-        quantise(0)
+        w_quantise(2)
+        w_quantise(3)
+        quantise(0, [(0, 2), (2, 4)])
 
-        for i in range(1, len(GROUPS) + 1):
-            now = GROUPS[i] if i < len(GROUPS) else []
-            after = GROUPS[i + 1] if i + 1 < len(GROUPS) else []
-            for q in now:
+        for i in range(1, NG + 1):
+            if i < NG:
                 for n in range(G):
-                    transposes(q, n)
-            for q in now:
-                copies(q, False)
-            for q in GROUPS[i - 1]:
-                passes(q)
-            for q in after:
-                sort_whole(q)
-            for q in now:
-                quantise(q)
-            for q in GROUPS[i - 1]:
-                results(q)
+                    transposes(i, n)
+            if i > 1:
+                quantise(i - 1, [(0, G)])
+            if i + 1 < NG:
+                sort_whole(i + 1)
+            if i < NG:
+                copies(i)
+            passes(i - 1)
+            results(i - 1)

@@ -39,7 +39,7 @@ def tile_stebitlinear_t_kernel(tc, x, sign_weights, scales, out):
         spool = ctx.enter_context(tc.tile_pool(name="spool", bufs=3))
         gpool = ctx.enter_context(tc.tile_pool(name="gpool", bufs=3))
         cpool = ctx.enter_context(tc.tile_pool(name="cpool", bufs=4))
-        opool = ctx.enter_context(tc.tile_pool(name="opool", bufs=4))
+        opool = ctx.enter_context(tc.tile_pool(name="opool", bufs=7))
         psum = ctx.enter_context(tc.psum_pool(name="psum", bufs=8))
 
         ident = const.tile([P, P], F32)
@@ -58,7 +58,7 @@ def tile_stebitlinear_t_kernel(tc, x, sign_weights, scales, out):
         def load(h):
             x_sb = xpool.tile([P, J, K], BF16, name="x_sb")
             xt[h] = x_sb
-            pieces = [(0, 2), (2, 4), (4, 8)] if h == 0 else [(0, J)]
+            pieces = {0: [(0, 2), (2, 4), (4, 8)], 1: [(0, 4), (4, 8)], 2: [(0, 4), (4, 8)]}.get(h, [(0, J)])
             for (a, b) in pieces:
                 nc.sync.dma_start(out=x_sb[:, a:b, :], in_=xv[h, :, a:b, :])
 
@@ -212,8 +212,7 @@ def tile_stebitlinear_t_kernel(tc, x, sign_weights, scales, out):
                 if k == stage["width"] - 1:
                     h = stage["first"] // J
                     j0 = stage["first"] % J
-                    queue = nc.sync if at_end else nc.scalar
-                    queue.dma_start(out=ov[h, :, j0:j0 + k + 1, :], in_=o_sb[:, 0:k + 1, :])
+                    nc.sync.dma_start(out=ov[h, :, j0:j0 + k + 1, :], in_=o_sb[:, 0:k + 1, :])
 
         for t in range(4):
             w_sign(t)
@@ -247,9 +246,13 @@ def tile_stebitlinear_t_kernel(tc, x, sign_weights, scales, out):
                     transposes(i, n)
             if i > 1:
                 quantise(i - 1, [(0, G)])
-            if i + 1 < NG:
-                sort_whole(i + 1)
-            if i < NG:
+            if i == 1:
                 copies(i)
+                sort_whole(i + 1)
+            else:
+                if i + 1 < NG:
+                    sort_whole(i + 1)
+                if i < NG:
+                    copies(i)
             passes(i - 1)
             results(i - 1)

@@ -20,10 +20,12 @@ TOK = 8192
 TILES = TOK // P
 J = 8
 NCH = TILES // J
-G = 4
-NG = TILES // G
 XB = 4
+U = 4
+UNITS = [2, 2] + [4] * 14 + [2, 2]
+GROUPS = [1] * 18
 STORE_UNITS = [4] * 15 + [2, 1, 1]
+TINY = 2.0 ** -7
 
 
 def tile_stebitlinear_t_kernel(tc, x, sign_weights, scales, out):
@@ -34,10 +36,9 @@ def tile_stebitlinear_t_kernel(tc, x, sign_weights, scales, out):
     with ExitStack() as ctx:
         ctx.enter_context(tc.manual_schedule())
         const = ctx.enter_context(tc.tile_pool(name="const", bufs=1))
-        wprep = ctx.enter_context(tc.tile_pool(name="wprep", bufs=1))
         xpool = ctx.enter_context(tc.tile_pool(name="xpool", bufs=XB))
-        spool = ctx.enter_context(tc.tile_pool(name="spool", bufs=3))
-        gpool = ctx.enter_context(tc.tile_pool(name="gpool", bufs=3))
+        spool = ctx.enter_context(tc.tile_pool(name="spool", bufs=4))
+        gpool = ctx.enter_context(tc.tile_pool(name="gpool", bufs=4))
         cpool = ctx.enter_context(tc.tile_pool(name="cpool", bufs=4))
         opool = ctx.enter_context(tc.tile_pool(name="opool", bufs=7))
         psum = ctx.enter_context(tc.psum_pool(name="psum", bufs=8))
@@ -46,12 +47,12 @@ def tile_stebitlinear_t_kernel(tc, x, sign_weights, scales, out):
         masks.make_identity(nc, ident[:])
 
         sc = const.tile([P, 4, 16], BF16)
-        nc.sync.dma_start(out=sc[:, :, 0:8], in_=scales.rearrange("(t p g) -> p t g", t=4, p=P))
         scf = const.tile([P, 4, 8], F32)
+        sw = opool.tile([P, 4, K], BF16, tag="o", name="sw")
+        nc.sync.dma_start(out=sc[:, :, 0:8], in_=scales.rearrange("(t p g) -> p t g", t=4, p=P))
         nc.vector.tensor_copy(out=scf[:], in_=sc[:, :, 0:8])
-        sw = wprep.tile([P, 4, K], BF16)
-        for t in range(4):
-            nc.sync.dma_start(out=sw[:, t, :], in_=sign_weights[t * P:(t + 1) * P, :])
+        scb = const.tile([P, 4, 8], F32)
+        nc.vector.tensor_scalar_mul(out=scb[:], in0=scf[:], scalar1=1.0 / TINY)
 
         xt = {}
 
@@ -62,50 +63,80 @@ def tile_stebitlinear_t_kernel(tc, x, sign_weights, scales, out):
             for (a, b) in pieces:
                 nc.sync.dma_start(out=x_sb[:, a:b, :], in_=xv[h, :, a:b, :])
 
+        for t in range(4):
+            nc.sync.dma_start(out=sw[:, t, :], in_=sign_weights[t * P:(t + 1) * P, :])
         for h in range(XB):
             load(h)
 
-        gw = wprep.tile([P, 2 * O * 4], BF16, align_bytes=64)
+        gw = gpool.tile([P, 2 * O * 4], BF16, tag="g", align_bytes=64, name="gw")
         gwf = gw[:].bitcast(F32).rearrange("p (c t r u) -> p c t r u", c=2, t=4, u=2)
         w_codes = const.tile([P, 2 * O], U32, align_bytes=64)
         w_scl = const.tile([P, 2 * O], U8, align_bytes=64)
-        sg_of = {}
+        sgn = opool.tile([P, 4, K], BF16, tag="o", name="sgn")
+        srt_w = opool.tile([P, 4, 2, 2, 2 * P], BF16, tag="o", name="srt_w")
+        low = opool.tile([P, 4, K], BF16, tag="o", name="low")
+        clamped = set()
         wt_of = {}
 
         def w_sign(t):
-            sg = wprep.tile([P, K], BF16, tag="sg", bufs=4, name="sg")
-            nc.scalar.activation(out=sg[:], in_=sw[:, t, :], func=ACT.Sign)
-            sg_of[t] = sg
+            nc.scalar.activation(out=sgn[:, t, :], in_=sw[:, t, :], func=ACT.Sign)
 
-        def w_scale_and_transpose(t):
-            ws = wprep.tile([P, 2, 2, 2 * P], BF16, tag="ws", bufs=4, name="ws")
+        def w_clamp(a, b):
+            nc.vector.tensor_scalar(
+                out=low[:, a:b, :], in0=sw[:, a:b, :], scalar1=1.0, scalar2=-1.0, op0=ALU.min, op1=ALU.max)
+            nc.vector.tensor_scalar(
+                out=sgn[:, a:b, :], in0=low[:, a:b, :], scalar1=2.0 ** 126, scalar2=-TINY, op0=ALU.mult, op1=ALU.max)
+            for t in range(a, b):
+                clamped.add(t)
+
+        def w_scale(t):
             for g in range(8):
                 c = g // 4
                 a0 = (g % 4) * 64
-                nc.vector.tensor_scalar_mul(
-                    out=ws[:, c, :, a0:a0 + 64].rearrange("p u (a i) -> p a u i", i=16),
-                    in0=sg_of[t][:, g * P:(g + 1) * P].rearrange("p (a u i) -> p a u i", u=2, i=16),
-                    scalar1=scf[:, t, g:g + 1],
-                )
-            wv = ws[:].bitcast(F32)
+                dst = srt_w[:, t, c, :, a0:a0 + 64].rearrange("p u (a i) -> p a u i", i=16)
+                src = sgn[:, t, g * P:(g + 1) * P].rearrange("p (a u i) -> p a u i", u=2, i=16)
+                if t in clamped:
+                    nc.vector.tensor_scalar(
+                        out=dst, in0=src, scalar1=TINY, scalar2=scb[:, t, g:g + 1], op0=ALU.min, op1=ALU.mult)
+                else:
+                    nc.vector.tensor_scalar_mul(out=dst, in0=src, scalar1=scf[:, t, g:g + 1])
+
+        def w_transpose(t):
+            wv = srt_w[:, t].bitcast(F32)
             w_t = psum.tile([P, 2, 2, P], F32, tag="bank", name="w_t")
             for c in range(2):
                 for u in range(2):
                     nc.tensor.transpose(w_t[:, c, u, :], wv[:, c, u, :], ident[:])
             wt_of[t] = w_t
 
-        def w_copy(t):
-            nc.scalar.copy(out=gwf[:, :, t, :, :], in_=wt_of[t][:].rearrange("p c u r -> p c r u"))
+        def w_copy(t, on_vector=False):
+            src = wt_of[t][:].rearrange("p c u r -> p c r u")
+            if on_vector:
+                nc.vector.tensor_copy(out=gwf[:, :, t, :, :], in_=src)
+            else:
+                nc.scalar.copy(out=gwf[:, :, t, :, :], in_=src)
 
-        def w_quantise(t):
-            for c in range(2):
-                first = c * O + t * P
-                nc.vector.quantize_mx(
-                    out=w_codes[:, first:first + P].bitcast(FP8X4),
-                    scales=w_scl[:, first:first + P],
-                    in_=gw[:, first * 4:(first + P) * 4],
-                )
+        def w_quantise(c, a, b):
+            first = c * O + a * P
+            last = c * O + b * P
+            nc.vector.quantize_mx(
+                out=w_codes[:, first:last].bitcast(FP8X4),
+                scales=w_scl[:, first:last],
+                in_=gw[:, first * 4:last * 4],
+            )
 
+        first_tile = []
+        s = 0
+        for size in UNITS:
+            first_tile.append(s)
+            s += size
+        assert s == TILES
+        groups = []
+        s = 0
+        for size in GROUPS:
+            groups.append(list(range(s, s + size)))
+            s += size
+        assert s == len(UNITS)
         srt_of = {}
         bank_of = {}
         grp_of = {}
@@ -113,64 +144,56 @@ def tile_stebitlinear_t_kernel(tc, x, sign_weights, scales, out):
         acc_of = {}
         next_load = [XB]
 
-        def sort(g, pieces):
-            h = (g * G) // J
-            j0 = (g * G) % J
-            srt = spool.tile([P, G * 2, 2, 2 * P], BF16, name="srt")
-            srt_of[g] = srt[:].bitcast(F32)
-            moves = []
-            for (a, b) in pieces:
-                moves.append((
-                    srt[:, 2 * a:2 * b, :, :].rearrange("p m u (a i) -> p m u a i", i=16),
-                    xt[h][:, j0 + a:j0 + b, :].rearrange(
-                        "p n (c a u i) -> p (n c) u a i", c=2, u=2, i=16),
-                ))
-            return moves
-
-        def sort_whole(g):
-            for (dst, src) in sort(g, [(0, G)]):
-                nc.vector.tensor_copy(out=dst, in_=src)
-            if (g * G + G) % J == 0 and next_load[0] < NCH:
+        def sort(v):
+            size = UNITS[v]
+            h = first_tile[v] // J
+            j0 = first_tile[v] % J
+            srt = spool.tile([P, U * 2, 2, 2 * P], BF16, tag="s", name="srt")
+            srt_of[v] = srt[:].bitcast(F32)
+            nc.vector.tensor_copy(
+                out=srt[:, 0:2 * size, :, :].rearrange("p m u (a i) -> p m u a i", i=16),
+                in_=xt[h][:, j0:j0 + size, :].rearrange("p n (c a u i) -> p (n c) u a i", c=2, u=2, i=16),
+            )
+            if j0 + size == J and next_load[0] < NCH:
                 load(next_load[0])
                 next_load[0] += 1
 
-        def transposes(g, n):
-            bank = psum.tile([P, 2, 2, P], F32, tag="bank", name="bank")
-            for c in range(2):
-                for u in range(2):
-                    nc.tensor.transpose(bank[:, c, u, :], srt_of[g][:, n * 2 + c, u, :], ident[:])
-            bank_of[(g, n)] = bank
+        def transposes(v):
+            for n in range(UNITS[v]):
+                bank = psum.tile([P, 2, 2, P], F32, tag="bank", name="bank")
+                for c in range(2):
+                    for u in range(2):
+                        nc.tensor.transpose(bank[:, c, u, :], srt_of[v][:, n * 2 + c, u, :], ident[:])
+                bank_of[(v, n)] = bank
 
-        def copy_out(g, n, on_vector):
-            if n == 0:
-                grp = gpool.tile([P, G * K], BF16, align_bytes=64, name="grp")
-                grp_of[g] = grp
-            gf = grp_of[g][:].bitcast(F32).rearrange("p (n c r u) -> p n c r u", n=G, c=2, u=2)
-            src = bank_of[(g, n)][:].rearrange("p c u r -> p c r u")
+        def copy_out(v, n, on_vector):
+            if v not in grp_of:
+                grp_of[v] = gpool.tile([P, U * K], BF16, tag="g", align_bytes=64, name="grp")
+            gf = grp_of[v][:].bitcast(F32).rearrange("p (n c r u) -> p n c r u", n=U, c=2, u=2)
+            src = bank_of[(v, n)][:].rearrange("p c u r -> p c r u")
             if on_vector:
                 nc.vector.tensor_copy(out=gf[:, n], in_=src)
             else:
                 nc.scalar.copy(out=gf[:, n], in_=src)
 
-        def copies(g):
-            for n in range(G):
-                copy_out(g, n, n % 2 == 0)
+        def copies(v, scalar_only=False):
+            for n in range(UNITS[v]):
+                copy_out(v, n, n % 2 == 0 and not scalar_only)
 
-        def quantise(g, pieces):
-            codes = cpool.tile([P, G * 2 * P], U32, align_bytes=64, name="codes")
-            scl = cpool.tile([P, G * 2 * P], U8, align_bytes=64, name="scl")
-            for (a, b) in pieces:
-                nc.vector.quantize_mx(
-                    out=codes[:, a * 2 * P:b * 2 * P].bitcast(FP8X4),
-                    scales=scl[:, a * 2 * P:b * 2 * P],
-                    in_=grp_of[g][:, a * K:b * K],
-                )
-            code_of[g] = (codes, scl)
+        def quantise(v):
+            size = UNITS[v]
+            codes = cpool.tile([P, U * 2 * P], U32, align_bytes=64, name="codes")
+            scl = cpool.tile([P, U * 2 * P], U8, align_bytes=64, name="scl")
+            nc.vector.quantize_mx(
+                out=codes[:, 0:size * 2 * P].bitcast(FP8X4),
+                scales=scl[:, 0:size * 2 * P],
+                in_=grp_of[v][:, 0:size * K],
+            )
+            code_of[v] = (codes, scl)
 
-        def passes(g):
-            codes, scl = code_of[g]
-            accs = []
-            for n in range(G):
+        def passes(v):
+            codes, scl = code_of[v]
+            for n in range(UNITS[v]):
                 acc = psum.tile([P, O], F32, tag="bank", name="acc")
                 for c in range(2):
                     cols = slice((n * 2 + c) * P, (n * 2 + c + 1) * P)
@@ -183,8 +206,7 @@ def tile_stebitlinear_t_kernel(tc, x, sign_weights, scales, out):
                         start=(c == 0),
                         stop=(c == 1),
                     )
-                accs.append(acc)
-            acc_of[g] = accs
+                acc_of[(v, n)] = acc
 
         unit_start = []
         s = 0
@@ -194,65 +216,70 @@ def tile_stebitlinear_t_kernel(tc, x, sign_weights, scales, out):
         assert s == TILES
         stage = {}
 
-        def results(g):
-            for n in range(G):
-                tile_no = g * G + n
+        def results(v):
+            for n in range(UNITS[v]):
+                tile_no = first_tile[v] + n
                 if tile_no in unit_start:
-                    o_sb = opool.tile([P, 4, O], F32, name="o_sb")
+                    o_sb = opool.tile([P, 4, O], F32, tag="o", name="o_sb")
                     stage["tile"] = o_sb
                     stage["first"] = tile_no
                     stage["width"] = STORE_UNITS[unit_start.index(tile_no)]
                 o_sb = stage["tile"]
                 k = tile_no - stage["first"]
-                at_end = tile_no >= TILES - 4
-                if at_end and n % 2 == 0:
-                    nc.vector.tensor_copy(out=o_sb[:, k, :], in_=acc_of[g][n][:])
+                if tile_no >= TILES - 4 and tile_no % 2 == 0:
+                    nc.vector.tensor_copy(out=o_sb[:, k, :], in_=acc_of[(v, n)][:])
                 else:
-                    nc.scalar.copy(out=o_sb[:, k, :], in_=acc_of[g][n][:])
+                    nc.scalar.copy(out=o_sb[:, k, :], in_=acc_of[(v, n)][:])
                 if k == stage["width"] - 1:
                     h = stage["first"] // J
                     j0 = stage["first"] % J
                     nc.sync.dma_start(out=ov[h, :, j0:j0 + k + 1, :], in_=o_sb[:, 0:k + 1, :])
 
-        for t in range(4):
-            w_sign(t)
-        for t in range(3):
-            w_scale_and_transpose(t)
-        halves = sort(0, [(0, 2), (2, 4)])
-        nc.vector.tensor_copy(out=halves[0][0], in_=halves[0][1])
-        transposes(0, 0)
-        transposes(0, 1)
-        w_scale_and_transpose(3)
-        nc.vector.tensor_copy(out=halves[1][0], in_=halves[1][1])
-        transposes(0, 2)
-        transposes(0, 3)
-        for t in range(3):
-            w_copy(t)
-        copy_out(0, 0, False)
-        copy_out(0, 1, False)
-        w_copy(3)
-        copy_out(0, 2, False)
-        copy_out(0, 3, False)
-        w_quantise(0)
-        w_quantise(1)
-        sort_whole(1)
-        w_quantise(2)
-        w_quantise(3)
-        quantise(0, [(0, 2), (2, 4)])
+        def w_quantise_tile(t):
+            for c in range(2):
+                w_quantise(c, t, t + 1)
 
-        for i in range(1, NG + 1):
-            if i < NG:
-                for n in range(G):
-                    transposes(i, n)
+        w_sign(1)
+        w_sign(2)
+        w_clamp(0, 1)
+        w_scale(0)
+        w_transpose(0)
+        w_clamp(3, 4)
+        w_scale(3)
+        w_transpose(3)
+        w_scale(1)
+        w_transpose(1)
+        w_copy(0)
+        w_copy(3)
+        sort(0)
+        w_scale(2)
+        transposes(0)
+        w_transpose(2)
+        w_copy(1)
+        copy_out(0, 0, True)
+        copy_out(0, 1, False)
+        w_copy(2)
+        w_quantise_tile(0)
+        w_quantise_tile(3)
+        sort(1)
+        w_quantise_tile(1)
+        quantise(0)
+        w_quantise_tile(2)
+
+        for i in range(1, len(groups) + 1):
+            if i < len(groups):
+                for v in groups[i]:
+                    transposes(v)
             if i > 1:
-                quantise(i - 1, [(0, G)])
-            if i == 1:
-                copies(i)
-                sort_whole(i + 1)
-            else:
-                if i + 1 < NG:
-                    sort_whole(i + 1)
-                if i < NG:
-                    copies(i)
-            passes(i - 1)
-            results(i - 1)
+                for v in groups[i - 1]:
+                    quantise(v)
+            if i + 1 < len(groups):
+                for v in groups[i + 1]:
+                    sort(v)
+            if i < len(groups):
+                for v in groups[i]:
+                    copies(v)
+            for v in groups[i - 1]:
+                passes(v)
+            for v in groups[i - 1]:
+                results(v)

@@ -23,8 +23,9 @@ NCH = TILES // J
 XB = 4
 U = 4
 UNITS = [2, 2] + [4] * 14 + [2, 2]
-GROUPS = [1] * 18
+GROUPS = [1, 1, 1] + [2] * 6 + [1] * 3
 STORE_UNITS = [4] * 15 + [2, 1, 1]
+VSHARE = {1: (), 2: (0,), 3: (0,), 4: (0,)}
 TINY = 2.0 ** -7
 
 
@@ -178,7 +179,7 @@ def tile_stebitlinear_t_kernel(tc, x, sign_weights, scales, out):
 
         def copies(v, scalar_only=False):
             for n in range(UNITS[v]):
-                copy_out(v, n, n % 2 == 0 and not scalar_only)
+                copy_out(v, n, n in VSHARE.get(v, (0, 2)))
 
         def quantise(v):
             size = UNITS[v]
@@ -270,16 +271,13 @@ def tile_stebitlinear_t_kernel(tc, x, sign_weights, scales, out):
             if i < len(groups):
                 for v in groups[i]:
                     transposes(v)
-            if i > 1:
-                for v in groups[i - 1]:
-                    quantise(v)
+                    copies(v)
             if i + 1 < len(groups):
                 for v in groups[i + 1]:
                     sort(v)
             if i < len(groups):
                 for v in groups[i]:
-                    copies(v)
+                    quantise(v)
             for v in groups[i - 1]:
                 passes(v)
-            for v in groups[i - 1]:
                 results(v)

@@ -70,7 +70,7 @@ def tile_stebitlinear_t_kernel(tc, x, sign_weights, scales, out):
             load(h)
 
         gw = gpool.tile([P, 2 * O * 4], BF16, tag="g", align_bytes=64, name="gw")
-        gwf = gw[:].bitcast(F32).rearrange("p (c t r u) -> p c t r u", c=2, t=4, u=2)
+        gwf = gw[:].bitcast(F32).rearrange("p (t c r u) -> p t c r u", t=4, c=2, u=2)
         w_codes = const.tile([P, 2 * O], U32, align_bytes=64)
         w_scl = const.tile([P, 2 * O], U8, align_bytes=64)
         sgn = opool.tile([P, 4, K], BF16, tag="o", name="sgn")
@@ -113,18 +113,9 @@ def tile_stebitlinear_t_kernel(tc, x, sign_weights, scales, out):
         def w_copy(t, on_vector=False):
             src = wt_of[t][:].rearrange("p c u r -> p c r u")
             if on_vector:
-                nc.vector.tensor_copy(out=gwf[:, :, t, :, :], in_=src)
+                nc.vector.tensor_copy(out=gwf[:, t], in_=src)
             else:
-                nc.scalar.copy(out=gwf[:, :, t, :, :], in_=src)
-
-        def w_quantise(c, a, b):
-            first = c * O + a * P
-            last = c * O + b * P
-            nc.vector.quantize_mx(
-                out=w_codes[:, first:last].bitcast(FP8X4),
-                scales=w_scl[:, first:last],
-                in_=gw[:, first * 4:last * 4],
-            )
+                nc.scalar.copy(out=gwf[:, t], in_=src)
 
         first_tile = []
         s = 0
@@ -238,7 +229,12 @@ def tile_stebitlinear_t_kernel(tc, x, sign_weights, scales, out):
 
         def w_quantise_tile(t):
             for c in range(2):
-                w_quantise(c, t, t + 1)
+                first = c * O + t * P
+                nc.vector.quantize_mx(
+                    out=w_codes[:, first:first + P].bitcast(FP8X4),
+                    scales=w_scl[:, first:first + P],
+                    in_=gw[:, (2 * t + c) * O:(2 * t + c + 1) * O],
+                )
 
         w_sign(1)
         w_sign(2)
@@ -257,12 +253,14 @@ def tile_stebitlinear_t_kernel(tc, x, sign_weights, scales, out):
         transposes(0)
         w_transpose(2)
         w_copy(1)
-        copy_out(0, 0, True)
+        copy_out(0, 0, False)
         copy_out(0, 1, False)
         w_copy(2)
+        sort(1)
+        transposes(1)
+        copies(1)
         w_quantise_tile(0)
         w_quantise_tile(3)
-        sort(1)
         w_quantise_tile(1)
         quantise(0)
         w_quantise_tile(2)
@@ -270,8 +268,9 @@ def tile_stebitlinear_t_kernel(tc, x, sign_weights, scales, out):
         for i in range(1, len(groups) + 1):
             if i < len(groups):
                 for v in groups[i]:
-                    transposes(v)
-                    copies(v)
+                    if i > 1:
+                        transposes(v)
+                        copies(v)
             if i + 1 < len(groups):
                 for v in groups[i + 1]:
                     sort(v)

@@ -47,13 +47,10 @@ def tile_stebitlinear_t_kernel(tc, x, sign_weights, scales, out):
         ident = const.tile([P, P], F32)
         masks.make_identity(nc, ident[:])
 
-        sc = const.tile([P, 4, 16], BF16)
+        sc = const.tile([P, 4, 8], BF16)
         scf = const.tile([P, 4, 8], F32)
         sw = opool.tile([P, 4, K], BF16, tag="o", name="sw")
-        nc.sync.dma_start(out=sc[:, :, 0:8], in_=scales.rearrange("(t p g) -> p t g", t=4, p=P))
-        nc.vector.tensor_copy(out=scf[:], in_=sc[:, :, 0:8])
         scb = const.tile([P, 4, 8], F32)
-        nc.vector.tensor_scalar_mul(out=scb[:], in0=scf[:], scalar1=1.0 / TINY)
 
         xt = {}
 
@@ -64,8 +61,11 @@ def tile_stebitlinear_t_kernel(tc, x, sign_weights, scales, out):
             for (a, b) in pieces:
                 nc.sync.dma_start(out=x_sb[:, a:b, :], in_=xv[h, :, a:b, :])
 
-        for t in range(4):
-            nc.sync.dma_start(out=sw[:, t, :], in_=sign_weights[t * P:(t + 1) * P, :])
+        swv = sign_weights.rearrange("(p t) k -> p t k", t=4)
+        nc.sync.dma_start(out=sw[:, 0:1, :], in_=swv[:, 0:1, :])
+        nc.sync.dma_start(out=sc[:], in_=scales.rearrange("(p t g) -> p t g", p=P, t=4))
+        nc.sync.dma_start(out=sw[:, 1:2, :], in_=swv[:, 1:2, :])
+        nc.sync.dma_start(out=sw[:, 2:4, :], in_=swv[:, 2:4, :])
         for h in range(XB):
             load(h)
 
@@ -89,6 +89,10 @@ def tile_stebitlinear_t_kernel(tc, x, sign_weights, scales, out):
                 out=sgn[:, a:b, :], in0=low[:, a:b, :], scalar1=2.0 ** 126, scalar2=-TINY, op0=ALU.mult, op1=ALU.max)
             for t in range(a, b):
                 clamped.add(t)
+
+        def w_factors():
+            nc.vector.tensor_copy(out=scf[:], in_=sc[:])
+            nc.vector.tensor_scalar_mul(out=scb[:], in0=scf[:], scalar1=1.0 / TINY)
 
         def w_scale(t):
             for g in range(8):
@@ -218,10 +222,12 @@ def tile_stebitlinear_t_kernel(tc, x, sign_weights, scales, out):
                     stage["width"] = STORE_UNITS[unit_start.index(tile_no)]
                 o_sb = stage["tile"]
                 k = tile_no - stage["first"]
+                dst = o_sb[:, k, :].rearrange("p (r t) -> p r t", t=4)
+                src = acc_of[(v, n)][:].rearrange("p (t r) -> p r t", t=4)
                 if tile_no >= TILES - 4 and tile_no % 2 == 0:
-                    nc.vector.tensor_copy(out=o_sb[:, k, :], in_=acc_of[(v, n)][:])
+                    nc.vector.tensor_copy(out=dst, in_=src)
                 else:
-                    nc.scalar.copy(out=o_sb[:, k, :], in_=acc_of[(v, n)][:])
+                    nc.scalar.copy(out=dst, in_=src)
                 if k == stage["width"] - 1:
                     h = stage["first"] // J
                     j0 = stage["first"] % J
@@ -239,6 +245,7 @@ def tile_stebitlinear_t_kernel(tc, x, sign_weights, scales, out):
         w_sign(1)
         w_sign(2)
         w_clamp(0, 1)
+        w_factors()
         w_scale(0)
         w_transpose(0)
         w_clamp(3, 4)

@@ -24,7 +24,7 @@ XB = 4
 U = 4
 UNITS = [2, 2] + [4] * 14 + [2, 2]
 GROUPS = [1, 1, 1] + [2] * 6 + [1] * 3
-STORE_UNITS = [4] * 15 + [2, 1, 1]
+STORE_UNITS = [8] * 5 + [4] * 5 + [2, 1, 1]
 VSHARE = {1: (), 2: (0,), 3: (0,), 4: (0,)}
 TINY = 2.0 ** -7
 
@@ -41,7 +41,7 @@ def tile_stebitlinear_t_kernel(tc, x, sign_weights, scales, out):
         spool = ctx.enter_context(tc.tile_pool(name="spool", bufs=4))
         gpool = ctx.enter_context(tc.tile_pool(name="gpool", bufs=4))
         cpool = ctx.enter_context(tc.tile_pool(name="cpool", bufs=4))
-        opool = ctx.enter_context(tc.tile_pool(name="opool", bufs=7))
+        opool = ctx.enter_context(tc.tile_pool(name="opool", bufs=5))
         psum = ctx.enter_context(tc.psum_pool(name="psum", bufs=8))
 
         ident = const.tile([P, P], F32)
@@ -57,7 +57,7 @@ def tile_stebitlinear_t_kernel(tc, x, sign_weights, scales, out):
         def load(h):
             x_sb = xpool.tile([P, J, K], BF16, name="x_sb")
             xt[h] = x_sb
-            pieces = {0: [(0, 2), (2, 4), (4, 8)], 1: [(0, 4), (4, 8)], 2: [(0, 4), (4, 8)]}.get(h, [(0, J)])
+            pieces = {0: [(0, 2), (2, 4), (4, 8)]}.get(h, [(0, J)])
             for (a, b) in pieces:
                 nc.sync.dma_start(out=x_sb[:, a:b, :], in_=xv[h, :, a:b, :])
 
@@ -216,7 +216,7 @@ def tile_stebitlinear_t_kernel(tc, x, sign_weights, scales, out):
             for n in range(UNITS[v]):
                 tile_no = first_tile[v] + n
                 if tile_no in unit_start:
-                    o_sb = opool.tile([P, 4, O], F32, tag="o", name="o_sb")
+                    o_sb = opool.tile([P, 8, O], F32, tag="o", name="o_sb")
                     stage["tile"] = o_sb
                     stage["first"] = tile_no
                     stage["width"] = STORE_UNITS[unit_start.index(tile_no)]

@@ -18,13 +18,13 @@ K = 1024
 O = 512
 TOK = 8192
 TILES = TOK // P
-J = 8
+J = 16
 NCH = TILES // J
-XB = 4
+XB = 3
 U = 4
 UNITS = [2, 2] + [4] * 14 + [2, 2]
 GROUPS = [1, 1, 1] + [2] * 6 + [1] * 3
-STORE_UNITS = [8] * 5 + [4] * 5 + [2, 1, 1]
+STORE_UNITS = [8] * 6 + [4] * 2 + [2, 2, 2, 2]
 VSHARE = {1: (), 2: (0,), 3: (0,), 4: (0,)}
 TINY = 2.0 ** -7
 
@@ -38,10 +38,10 @@ def tile_stebitlinear_t_kernel(tc, x, sign_weights, scales, out):
         ctx.enter_context(tc.manual_schedule())
         const = ctx.enter_context(tc.tile_pool(name="const", bufs=1))
         xpool = ctx.enter_context(tc.tile_pool(name="xpool", bufs=XB))
-        spool = ctx.enter_context(tc.tile_pool(name="spool", bufs=4))
-        gpool = ctx.enter_context(tc.tile_pool(name="gpool", bufs=4))
+        spool = ctx.enter_context(tc.tile_pool(name="spool", bufs=3))
+        gpool = ctx.enter_context(tc.tile_pool(name="gpool", bufs=3))
         cpool = ctx.enter_context(tc.tile_pool(name="cpool", bufs=4))
-        opool = ctx.enter_context(tc.tile_pool(name="opool", bufs=5))
+        opool = ctx.enter_context(tc.tile_pool(name="opool", bufs=4))
         psum = ctx.enter_context(tc.psum_pool(name="psum", bufs=8))
 
         ident = const.tile([P, P], F32)
@@ -57,7 +57,7 @@ def tile_stebitlinear_t_kernel(tc, x, sign_weights, scales, out):
         def load(h):
             x_sb = xpool.tile([P, J, K], BF16, name="x_sb")
             xt[h] = x_sb
-            pieces = {0: [(0, 2), (2, 4), (4, 8)]}.get(h, [(0, J)])
+            pieces = {0: [(0, 2), (2, 4), (4, 8), (8, 16)], 1: [(0, 8), (8, 16)]}.get(h, [(0, J)])
             for (a, b) in pieces:
                 nc.sync.dma_start(out=x_sb[:, a:b, :], in_=xv[h, :, a:b, :])
 
@@ -215,23 +215,25 @@ def tile_stebitlinear_t_kernel(tc, x, sign_weights, scales, out):
         def results(v):
             for n in range(UNITS[v]):
                 tile_no = first_tile[v] + n
-                if tile_no in unit_start:
+                if tile_no % 8 == 0:
                     o_sb = opool.tile([P, 8, O], F32, tag="o", name="o_sb")
                     stage["tile"] = o_sb
+                if tile_no in unit_start:
                     stage["first"] = tile_no
                     stage["width"] = STORE_UNITS[unit_start.index(tile_no)]
                 o_sb = stage["tile"]
-                k = tile_no - stage["first"]
+                k = tile_no % 8
                 dst = o_sb[:, k, :].rearrange("p (r t) -> p r t", t=4)
                 src = acc_of[(v, n)][:].rearrange("p (t r) -> p r t", t=4)
                 if tile_no >= TILES - 4 and tile_no % 2 == 0:
                     nc.vector.tensor_copy(out=dst, in_=src)
                 else:
                     nc.scalar.copy(out=dst, in_=src)
-                if k == stage["width"] - 1:
+                if tile_no == stage["first"] + stage["width"] - 1:
                     h = stage["first"] // J
                     j0 = stage["first"] % J
-                    nc.sync.dma_start(out=ov[h, :, j0:j0 + k + 1, :], in_=o_sb[:, 0:k + 1, :])
+                    w = stage["width"]
+                    nc.sync.dma_start(out=ov[h, :, j0:j0 + w, :], in_=o_sb[:, k + 1 - w:k + 1, :])
 
         def w_quantise_tile(t):
             for c in range(2):

from contextlib import ExitStack

import concourse.masks as masks
import concourse.mybir as mybir

FLOPS = 2 * 8192 * 1024 * 512

F32 = mybir.dt.float32
BF16 = mybir.dt.bfloat16
U32 = mybir.dt.uint32
U8 = mybir.dt.uint8
FP8X4 = mybir.dt.float8_e4m3fn_x4
ACT = mybir.ActivationFunctionType
ALU = mybir.AluOpType

P = 128
K = 1024
O = 512
TOK = 8192
TILES = TOK // P
J = 16
NCH = TILES // J
XB = 3
U = 4
UNITS = [2, 2] + [4] * 14 + [2, 2]
GROUPS = [1, 1, 1] + [2] * 6 + [1] * 3
STORE_UNITS = [8] * 6 + [4] * 2 + [2, 2, 2, 2]
VSHARE = {1: (), 2: (0,), 3: (0,), 4: (0,)}
TINY = 2.0 ** -7


def tile_stebitlinear_t_kernel(tc, x, sign_weights, scales, out):
    nc = tc.nc
    xv = x.flatten_outer_dims().rearrange("(h p j) k -> h p j k", p=P, j=J)
    ov = out.flatten_outer_dims().rearrange("(h p j) o -> h p j o", p=P, j=J)

    with ExitStack() as ctx:
        ctx.enter_context(tc.manual_schedule())
        const = ctx.enter_context(tc.tile_pool(name="const", bufs=1))
        xpool = ctx.enter_context(tc.tile_pool(name="xpool", bufs=XB))
        spool = ctx.enter_context(tc.tile_pool(name="spool", bufs=3))
        gpool = ctx.enter_context(tc.tile_pool(name="gpool", bufs=3))
        cpool = ctx.enter_context(tc.tile_pool(name="cpool", bufs=4))
        opool = ctx.enter_context(tc.tile_pool(name="opool", bufs=4))
        psum = ctx.enter_context(tc.psum_pool(name="psum", bufs=8))

        ident = const.tile([P, P], F32)
        masks.make_identity(nc, ident[:])

        sc = const.tile([P, 4, 8], BF16)
        scf = const.tile([P, 4, 8], F32)
        sw = opool.tile([P, 4, K], BF16, tag="o", name="sw")
        scb = const.tile([P, 4, 8], F32)

        xt = {}

        def load(h):
            x_sb = xpool.tile([P, J, K], BF16, name="x_sb")
            xt[h] = x_sb
            pieces = {0: [(0, 2), (2, 4), (4, 8), (8, 16)], 1: [(0, 8), (8, 16)]}.get(h, [(0, J)])
            for (a, b) in pieces:
                nc.sync.dma_start(out=x_sb[:, a:b, :], in_=xv[h, :, a:b, :])

        swv = sign_weights.rearrange("(p t) k -> p t k", t=4)
        nc.sync.dma_start(out=sw[:, 0:1, :], in_=swv[:, 0:1, :])
        nc.sync.dma_start(out=sc[:], in_=scales.rearrange("(p t g) -> p t g", p=P, t=4))
        nc.sync.dma_start(out=sw[:, 1:2, :], in_=swv[:, 1:2, :])
        nc.sync.dma_start(out=sw[:, 2:4, :], in_=swv[:, 2:4, :])
        for h in range(XB):
            load(h)

        gw = gpool.tile([P, 2 * O * 4], BF16, tag="g", align_bytes=64, name="gw")
        gwf = gw[:].bitcast(F32).rearrange("p (t c r u) -> p t c r u", t=4, c=2, u=2)
        w_codes = const.tile([P, 2 * O], U32, align_bytes=64)
        w_scl = const.tile([P, 2 * O], U8, align_bytes=64)
        sgn = opool.tile([P, 4, K], BF16, tag="o", name="sgn")
        srt_w = opool.tile([P, 4, 2, 2, 2 * P], BF16, tag="o", name="srt_w")
        low = opool.tile([P, 4, K], BF16, tag="o", name="low")
        clamped = set()
        wt_of = {}

        def w_sign(t):
            nc.scalar.activation(out=sgn[:, t, :], in_=sw[:, t, :], func=ACT.Sign)

        def w_clamp(a, b):
            nc.vector.tensor_scalar(
                out=low[:, a:b, :], in0=sw[:, a:b, :], scalar1=1.0, scalar2=-1.0, op0=ALU.min, op1=ALU.max)
            nc.vector.tensor_scalar(
                out=sgn[:, a:b, :], in0=low[:, a:b, :], scalar1=2.0 ** 126, scalar2=-TINY, op0=ALU.mult, op1=ALU.max)
            for t in range(a, b):
                clamped.add(t)

        def w_factors():
            nc.vector.tensor_copy(out=scf[:], in_=sc[:])
            nc.vector.tensor_scalar_mul(out=scb[:], in0=scf[:], scalar1=1.0 / TINY)

        def w_scale(t):
            for g in range(8):
                c = g // 4
                a0 = (g % 4) * 64
                dst = srt_w[:, t, c, :, a0:a0 + 64].rearrange("p u (a i) -> p a u i", i=16)
                src = sgn[:, t, g * P:(g + 1) * P].rearrange("p (a u i) -> p a u i", u=2, i=16)
                if t in clamped:
                    nc.vector.tensor_scalar(
                        out=dst, in0=src, scalar1=TINY, scalar2=scb[:, t, g:g + 1], op0=ALU.min, op1=ALU.mult)
                else:
                    nc.vector.tensor_scalar_mul(out=dst, in0=src, scalar1=scf[:, t, g:g + 1])

        def w_transpose(t):
            wv = srt_w[:, t].bitcast(F32)
            w_t = psum.tile([P, 2, 2, P], F32, tag="bank", name="w_t")
            for c in range(2):
                for u in range(2):
                    nc.tensor.transpose(w_t[:, c, u, :], wv[:, c, u, :], ident[:])
            wt_of[t] = w_t

        def w_copy(t, on_vector=False):
            src = wt_of[t][:].rearrange("p c u r -> p c r u")
            if on_vector:
                nc.vector.tensor_copy(out=gwf[:, t], in_=src)
            else:
                nc.scalar.copy(out=gwf[:, t], in_=src)

        first_tile = []
        s = 0
        for size in UNITS:
            first_tile.append(s)
            s += size
        assert s == TILES
        groups = []
        s = 0
        for size in GROUPS:
            groups.append(list(range(s, s + size)))
            s += size
        assert s == len(UNITS)
        srt_of = {}
        bank_of = {}
        grp_of = {}
        code_of = {}
        acc_of = {}
        next_load = [XB]

        def sort(v):
            size = UNITS[v]
            h = first_tile[v] // J
            j0 = first_tile[v] % J
            srt = spool.tile([P, U * 2, 2, 2 * P], BF16, tag="s", name="srt")
            srt_of[v] = srt[:].bitcast(F32)
            nc.vector.tensor_copy(
                out=srt[:, 0:2 * size, :, :].rearrange("p m u (a i) -> p m u a i", i=16),
                in_=xt[h][:, j0:j0 + size, :].rearrange("p n (c a u i) -> p (n c) u a i", c=2, u=2, i=16),
            )
            if j0 + size == J and next_load[0] < NCH:
                load(next_load[0])
                next_load[0] += 1

        def transposes(v):
            for n in range(UNITS[v]):
                bank = psum.tile([P, 2, 2, P], F32, tag="bank", name="bank")
                for c in range(2):
                    for u in range(2):
                        nc.tensor.transpose(bank[:, c, u, :], srt_of[v][:, n * 2 + c, u, :], ident[:])
                bank_of[(v, n)] = bank

        def copy_out(v, n, on_vector):
            if v not in grp_of:
                grp_of[v] = gpool.tile([P, U * K], BF16, tag="g", align_bytes=64, name="grp")
            gf = grp_of[v][:].bitcast(F32).rearrange("p (n c r u) -> p n c r u", n=U, c=2, u=2)
            src = bank_of[(v, n)][:].rearrange("p c u r -> p c r u")
            if on_vector:
                nc.vector.tensor_copy(out=gf[:, n], in_=src)
            else:
                nc.scalar.copy(out=gf[:, n], in_=src)

        def copies(v, scalar_only=False):
            for n in range(UNITS[v]):
                copy_out(v, n, n in VSHARE.get(v, (0, 2)))

        def quantise(v):
            size = UNITS[v]
            codes = cpool.tile([P, U * 2 * P], U32, align_bytes=64, name="codes")
            scl = cpool.tile([P, U * 2 * P], U8, align_bytes=64, name="scl")
            nc.vector.quantize_mx(
                out=codes[:, 0:size * 2 * P].bitcast(FP8X4),
                scales=scl[:, 0:size * 2 * P],
                in_=grp_of[v][:, 0:size * K],
            )
            code_of[v] = (codes, scl)

        def passes(v):
            codes, scl = code_of[v]
            for n in range(UNITS[v]):
                acc = psum.tile([P, O], F32, tag="bank", name="acc")
                for c in range(2):
                    cols = slice((n * 2 + c) * P, (n * 2 + c + 1) * P)
                    nc.tensor.matmul_mx(
                        out=acc[:],
                        lhsT=codes[:, cols].bitcast(FP8X4),
                        lhsT_scale=scl[:, cols],
                        rhs=w_codes[:, c * O:(c + 1) * O].bitcast(FP8X4),
                        rhs_scale=w_scl[:, c * O:(c + 1) * O],
                        start=(c == 0),
                        stop=(c == 1),
                    )
                acc_of[(v, n)] = acc

        unit_start = []
        s = 0
        for n_tiles in STORE_UNITS:
            unit_start.append(s)
            s += n_tiles
        assert s == TILES
        stage = {}

        def results(v):
            for n in range(UNITS[v]):
                tile_no = first_tile[v] + n
                if tile_no % 8 == 0:
                    o_sb = opool.tile([P, 8, O], F32, tag="o", name="o_sb")
                    stage["tile"] = o_sb
                if tile_no in unit_start:
                    stage["first"] = tile_no
                    stage["width"] = STORE_UNITS[unit_start.index(tile_no)]
                o_sb = stage["tile"]
                k = tile_no % 8
                dst = o_sb[:, k, :].rearrange("p (r t) -> p r t", t=4)
                src = acc_of[(v, n)][:].rearrange("p (t r) -> p r t", t=4)
                if tile_no >= TILES - 4 and tile_no % 2 == 0:
                    nc.vector.tensor_copy(out=dst, in_=src)
                else:
                    nc.scalar.copy(out=dst, in_=src)
                if tile_no == stage["first"] + stage["width"] - 1:
                    h = stage["first"] // J
                    j0 = stage["first"] % J
                    w = stage["width"]
                    nc.sync.dma_start(out=ov[h, :, j0:j0 + w, :], in_=o_sb[:, k + 1 - w:k + 1, :])

        def w_quantise_tile(t):
            for c in range(2):
                first = c * O + t * P
                nc.vector.quantize_mx(
                    out=w_codes[:, first:first + P].bitcast(FP8X4),
                    scales=w_scl[:, first:first + P],
                    in_=gw[:, (2 * t + c) * O:(2 * t + c + 1) * O],
                )

        w_sign(1)
        w_sign(2)
        w_clamp(0, 1)
        w_factors()
        w_scale(0)
        w_transpose(0)
        w_clamp(3, 4)
        w_scale(3)
        w_transpose(3)
        w_scale(1)
        w_transpose(1)
        w_copy(0)
        w_copy(3)
        sort(0)
        w_scale(2)
        transposes(0)
        w_transpose(2)
        w_copy(1)
        copy_out(0, 0, False)
        copy_out(0, 1, False)
        w_copy(2)
        sort(1)
        transposes(1)
        copies(1)
        w_quantise_tile(0)
        w_quantise_tile(3)
        w_quantise_tile(1)
        quantise(0)
        w_quantise_tile(2)

        for i in range(1, len(groups) + 1):
            if i < len(groups):
                for v in groups[i]:
                    if i > 1:
                        transposes(v)
                        copies(v)
            if i + 1 < len(groups):
                for v in groups[i + 1]:
                    sort(v)
            if i < len(groups):
                for v in groups[i]:
                    quantise(v)
            for v in groups[i - 1]:
                passes(v)
                results(v)
